import numpy as np
import ml_dtypes


def mxq(x, axis, fmt="e4m3"):
    dtype, down = {"e4m3": (ml_dtypes.float8_e4m3fn, 7), "e5m2": (ml_dtypes.float8_e5m2, 14)}[fmt]
    v = np.moveaxis(np.asarray(x, np.float32).astype(ml_dtypes.bfloat16).astype(np.float64), axis, -1)
    blocks = v.reshape(v.shape[:-1] + (-1, 32))
    amax = np.abs(blocks).max(-1, keepdims=True)
    byte = np.maximum(np.where(amax > 0, np.frexp(amax)[1] - 1 + 127, 0) - down, 1)
    scale = np.exp2(byte - 127.0)
    codes = (blocks / scale).astype(np.float32).astype(dtype).astype(np.float64)
    return np.moveaxis((codes * scale).reshape(v.shape), -1, axis)


WIDE = False


def mx_kscale(k):
    if not WIDE:
        return np.ones(k)
    levels = np.array([10, -10, 5, -5, 0])
    a = np.random.permutation(np.resize(levels, k // 512 * 4)).reshape(k // 512, 4)
    idx = np.arange(k)
    return np.exp2(a[idx // 512, idx % 128 // 32])


BF16 = ml_dtypes.bfloat16


def bf(x):
    return np.asarray(x, np.float32).astype(BF16)


def f64(x):
    return np.asarray(x).astype(np.float64)


E2M1 = np.array([0.0, 0.5, 1.0, 1.5, 2.0, 3.0, 4.0, 6.0, -0.0, -0.5, -1.0, -1.5, -2.0, -3.0, -4.0, -6.0])


def pack_weight(w, fmt):
    k, n = w.shape
    w = f64(bf(w)).reshape(k // 32, 32, n)
    amax = np.abs(w).max(1)
    if fmt == "e4m3":
        byte = np.frexp(amax)[1] - 1 + 127 - 7
    else:
        mant, ex = np.frexp(amax / 6.0)
        byte = np.where(mant > 0.5, ex, ex - 1) + 127
    byte = np.clip(np.where(amax > 0, byte, 1), 1, 254)
    scaled = (w * np.exp2(127.0 - byte)[:, None, :]).reshape(k, n).astype(np.float32)
    by_word = np.ascontiguousarray(scaled.reshape(k // 512, 128, 4, n).transpose(0, 1, 3, 2))
    if fmt == "e4m3":
        words = by_word.astype(ml_dtypes.float8_e4m3fn).view(np.uint8)
    else:
        c = by_word.astype(ml_dtypes.float4_e2m1fn).view(np.uint8) & 0xF
        words = c[..., 0::2] | (c[..., 1::2] << 4)
    return np.ascontiguousarray(words), np.ascontiguousarray(byte.astype(np.uint8).reshape(k // 512, 16, n))


def unpack_weight(words, scales, fmt):
    g, p, n, _ = words.shape
    if fmt == "e4m3":
        vals = np.ascontiguousarray(words).view(ml_dtypes.float8_e4m3fn).astype(np.float64)
    else:
        nib = np.empty((g, p, n, 4), np.uint8)
        nib[..., 0::2] = words & 0xF
        nib[..., 1::2] = words >> 4
        vals = E2M1[nib]
    vals = vals * np.repeat(np.exp2(scales.astype(np.float64) - 127.0), 8, axis=1)[..., None]
    return vals.transpose(0, 1, 3, 2).reshape(g * 512, n)


B, S, D, NH, NKV, HD = 1, 128, 8192, 16, 4, 128
ROPE_THETA = 10000.0
FMT = "e4m3"


def rope_tables():
    freqs = 1.0 / (ROPE_THETA ** (f64(np.arange(0, HD, 2)) / HD))
    ang = np.outer(f64(np.arange(S)), freqs)
    return np.cos(ang), np.sin(ang)


def rope(x, cos, sin):
    xr = x.reshape(*x.shape[:-1], HD // 2, 2)
    re, im = xr[..., 0], xr[..., 1]
    c = cos[None, :, None, :]
    s = sin[None, :, None, :]
    return np.stack((re * c - im * s, re * s + im * c), axis=-1).reshape(x.shape)


def setup_inputs():
    s = mx_kscale(D)
    hidden_states = bf(np.random.standard_normal((B, S, D)) * s)
    wq_words, wq_scales = pack_weight(np.random.standard_normal((D, NH * HD)) / np.sqrt(D) / s[:, None], FMT)
    wk_words, wk_scales = pack_weight(np.random.standard_normal((D, NKV * HD)) / np.sqrt(D) / s[:, None], FMT)
    wv_words, wv_scales = pack_weight(np.random.standard_normal((D, NKV * HD)) * 2.0 / np.sqrt(D) / s[:, None], FMT)
    return {"hidden_states": hidden_states,
            "wq_words": wq_words, "wq_scales": wq_scales,
            "wk_words": wk_words, "wk_scales": wk_scales,
            "wv_words": wv_words, "wv_scales": wv_scales}


def reference(hidden_states, wq_words, wq_scales, wk_words, wk_scales, wv_words, wv_scales):
    xq = mxq(f64(hidden_states), 2, "e4m3")
    q = (xq @ unpack_weight(wq_words, wq_scales, FMT)).reshape(B, S, NH, HD)
    k = (xq @ unpack_weight(wk_words, wk_scales, FMT)).reshape(B, S, NKV, HD)
    v = (xq @ unpack_weight(wv_words, wv_scales, FMT)).reshape(B, S, NKV, HD)
    cos, sin = rope_tables()
    return rope(q, cos, sin), rope(k, cos, sin), v

@@ -1,0 +1,255 @@
+import math
+from contextlib import ExitStack
+
+import concourse.mybir as mybir
+from concourse.masks import make_identity
+
+F32 = mybir.dt.float32
+BF16 = mybir.dt.bfloat16
+I32 = mybir.dt.int32
+U32 = mybir.dt.uint32
+U8 = mybir.dt.uint8
+FP8X4 = mybir.dt.float8_e4m3fn_x4
+ALU = mybir.AluOpType
+ACT = mybir.ActivationFunctionType
+
+P = 128
+PACK = 4
+K_PASS = P * PACK
+TOKENS = 128
+D_MODEL = 8192
+PASSES = D_MODEL // K_PASS
+WORDS_PER_PASS = K_PASS // 2
+N_TILE = 512
+HEAD = 128
+PAIRS = HEAD // 2
+HEADS_PER_TILE = N_TILE // HEAD
+Q_COLS = 2048
+Q_TILES = Q_COLS // N_TILE
+ROPE_THETA = 10000.0
+
+SCALE_ROWS = 4
+QUADRANTS = 4
+PLANES_PER_TILE = 4
+K_OFFSET = 0
+V_OFFSET = 4
+
+PASSES_PER_QUANTISE = 4
+ROUND_MAGIC = 12582912.0
+
+WQ_BUFS = 12
+KV_BUFS = 16
+
+FLOPS = 2 * TOKENS * D_MODEL * (Q_COLS + 2 * N_TILE)
+
+
+def build_rope_tables(nc, keep):
+    position = keep.tile([P, 1], F32)
+    nc.gpsimd.iota(
+        position[:], pattern=[[0, 1]], base=0, channel_multiplier=1, allow_small_or_imprecise_dtypes=True
+    )
+
+    ratio = ROPE_THETA ** (-2.0 / HEAD)
+    frequency = keep.tile([P, PAIRS], F32)
+    nc.vector.memset(frequency[:, 0:1], 1.0)
+    filled = 1
+    while filled < PAIRS:
+        nc.vector.tensor_scalar(
+            out=frequency[:, filled : 2 * filled],
+            in0=frequency[:, 0:filled],
+            scalar1=ratio**filled,
+            scalar2=None,
+            op0=ALU.mult,
+        )
+        filled *= 2
+
+    angle = keep.tile([P, PAIRS], F32)
+    nc.vector.tensor_scalar(
+        out=angle[:],
+        in0=frequency[:],
+        scalar1=position[:, 0:1],
+        scalar2=1.0 / (2.0 * math.pi),
+        op0=ALU.mult,
+        op1=ALU.mult,
+    )
+    whole = keep.tile([P, PAIRS], F32)
+    nc.vector.tensor_scalar(
+        out=whole[:], in0=angle[:], scalar1=ROUND_MAGIC, scalar2=ROUND_MAGIC, op0=ALU.add, op1=ALU.subtract
+    )
+    fraction = keep.tile([P, PAIRS], F32)
+    nc.vector.tensor_tensor(out=fraction[:], in0=angle[:], in1=whole[:], op=ALU.subtract)
+
+    sin_signed = keep.tile([P, 2, PAIRS], F32)
+    nc.scalar.activation(out=sin_signed[:, 0, :], in_=fraction[:], func=ACT.Sin, scale=-2.0 * math.pi)
+    nc.scalar.activation(out=sin_signed[:, 1, :], in_=fraction[:], func=ACT.Sin, scale=2.0 * math.pi)
+    sin_half = keep.tile([P, PAIRS], F32)
+    nc.scalar.activation(out=sin_half[:], in_=fraction[:], func=ACT.Sin, scale=math.pi)
+    return sin_signed, sin_half
+
+
+def finish_cos_table(nc, keep, sin_half):
+    sin_half_sq = keep.tile([P, PAIRS], F32)
+    nc.vector.tensor_tensor(out=sin_half_sq[:], in0=sin_half[:], in1=sin_half[:], op=ALU.mult)
+    cos_pairs = keep.tile([P, HEAD], F32)
+    nc.vector.tensor_scalar(
+        out=cos_pairs[:].rearrange("p (j e) -> p j e", e=2),
+        in0=sin_half_sq[:].unsqueeze(2).to_broadcast([P, PAIRS, 2]),
+        scalar1=-2.0,
+        scalar2=1.0,
+        op0=ALU.mult,
+        op1=ALU.add,
+    )
+    return cos_pairs
+
+
+def load_scale_planes(nc, keep, wq_scales, wk_scales, wv_scales):
+    q_planes = keep.tile([P, PASSES // PLANES_PER_TILE, Q_COLS], U8, align_bytes=64)
+    kv_planes = keep.tile([P, PASSES, N_TILE], U8, align_bytes=64)
+    nc.vector.memset(q_planes[:].bitcast(I32), 0)
+    nc.vector.memset(kv_planes[:].bitcast(I32), 0)
+
+    rows = PLANES_PER_TILE * SCALE_ROWS
+    for group in range(PASSES // PLANES_PER_TILE):
+        for quadrant in range(QUADRANTS):
+            nc.sync.dma_start(
+                out=q_planes[32 * quadrant : 32 * quadrant + rows, group, :].bitcast(I32),
+                in_=wq_scales[
+                    PLANES_PER_TILE * group : PLANES_PER_TILE * (group + 1),
+                    SCALE_ROWS * quadrant : SCALE_ROWS * (quadrant + 1),
+                    :,
+                ].bitcast(I32),
+            )
+    for scales, offset in ((wk_scales, K_OFFSET), (wv_scales, V_OFFSET)):
+        by_row = scales.rearrange("g (quadrant r) n -> r quadrant g n", r=SCALE_ROWS)
+        for r in range(SCALE_ROWS):
+            nc.sync.dma_start(
+                out=kv_planes[offset + r : P : 32, :, :].bitcast(I32),
+                in_=by_row[r].bitcast(I32),
+            )
+    return q_planes, kv_planes
+
+
+def quantise_x(nc, keep, transposed, x_sb, identity):
+    x_words = x_sb[:].bitcast(F32)
+    grouped = keep.tile([P, PASSES, TOKENS * PACK], BF16, align_bytes=64)
+    grouped_words = grouped[:].bitcast(F32)
+    x_codes = keep.tile([P, PASSES, TOKENS], U32, align_bytes=64)
+    x_planes = keep.tile([P, PASSES, TOKENS], U8, align_bytes=64)
+
+    for first in range(0, PASSES, PASSES_PER_QUANTISE):
+        for pair in range(first, first + PASSES_PER_QUANTISE, 2):
+            bank = transposed.tile([P, 2, 2, TOKENS], F32)
+            for a in range(2):
+                start = WORDS_PER_PASS * (pair + a)
+                for u in range(2):
+                    nc.tensor.transpose(
+                        bank[:, a, u, :], x_words[:, start + u : start + WORDS_PER_PASS : 2], identity[:]
+                    )
+            side_by_side = grouped_words[:, pair : pair + 2, :].rearrange("p a (t u) -> p a t u", u=2)
+            if pair % 4 == 0:
+                nc.vector.tensor_copy(out=side_by_side, in_=bank[:].rearrange("p a u t -> p a t u"))
+            else:
+                nc.scalar.copy(out=side_by_side, in_=bank[:].rearrange("p a u t -> p a t u"))
+        these = slice(first, first + PASSES_PER_QUANTISE)
+        nc.vector.quantize_mx(
+            out=x_codes[:, these, :].rearrange("p g t -> p (g t)").bitcast(FP8X4),
+            scales=x_planes[:, these, :].rearrange("p g t -> p (g t)"),
+            in_=grouped[:, these, :].rearrange("p g c -> p (g c)"),
+        )
+    return x_codes, x_planes
+
+
+def rotate(nc, work, acc, cos_pairs, sin_signed, rotated):
+    with_cos = work.tile([P, N_TILE], F32)
+    nc.vector.tensor_tensor(
+        out=with_cos[:].rearrange("p (h d) -> p h d", d=HEAD),
+        in0=acc[:].rearrange("p (h d) -> p h d", d=HEAD),
+        in1=cos_pairs[:].unsqueeze(1).to_broadcast([P, HEADS_PER_TILE, HEAD]),
+        op=ALU.mult,
+    )
+    acc_planes = acc[:].rearrange("p (h j e) -> p e h j", j=PAIRS, e=2)
+    with_sin = work.tile([P, 2, HEADS_PER_TILE, PAIRS], F32)
+    for e in range(2):
+        nc.vector.tensor_tensor(
+            out=with_sin[:, e, :, :],
+            in0=acc_planes[:, 1 - e, :, :],
+            in1=sin_signed[:, e, :].unsqueeze(1).to_broadcast([P, HEADS_PER_TILE, PAIRS]),
+            op=ALU.mult,
+        )
+    nc.vector.tensor_tensor(
+        out=rotated.rearrange("p (m e) -> p m e", e=2),
+        in0=with_cos[:].rearrange("p (m e) -> p m e", e=2),
+        in1=with_sin[:].rearrange("p e h j -> p (h j) e"),
+        op=ALU.add,
+    )
+
+
+def tile_rptattention_pa_k_kernel(
+    tc, hidden_states, wq_words, wq_scales, wk_words, wk_scales, wv_words, wv_scales, out_0, out_1, out_2
+):
+    nc = tc.nc
+    with ExitStack() as ctx:
+        ctx.enter_context(tc.manual_schedule())
+        keep = ctx.enter_context(tc.tile_pool(name="keep", bufs=1))
+        work = ctx.enter_context(tc.tile_pool(name="work", bufs=2))
+        wq_pool = ctx.enter_context(tc.tile_pool(name="wq", bufs=WQ_BUFS))
+        kv_pool = ctx.enter_context(tc.tile_pool(name="kv", bufs=KV_BUFS))
+        sums = ctx.enter_context(tc.psum_pool(name="sums", bufs=1))
+        transposed = ctx.enter_context(tc.psum_pool(name="transposed", bufs=2))
+
+        x_sb = keep.tile([P, D_MODEL], BF16)
+        nc.sync.dma_start(out=x_sb[:], in_=hidden_states.rearrange("b s d -> (b s) d"))
+        q_planes, kv_planes = load_scale_planes(nc, keep, wq_scales, wk_scales, wv_scales)
+
+        identity = keep.tile([P, P], F32)
+        make_identity(nc, identity[:])
+        sin_signed, sin_half = build_rope_tables(nc, keep)
+        x_codes, x_planes = quantise_x(nc, keep, transposed, x_sb, identity)
+        cos_pairs = finish_cos_table(nc, keep, sin_half)
+
+        def mx_pass(acc, g, words, plane):
+            nc.tensor.matmul_mx(
+                out=acc[:],
+                lhsT=x_codes[:, g, :].bitcast(FP8X4),
+                lhsT_scale=x_planes[:, g, :],
+                rhs=words.bitcast(FP8X4),
+                rhs_scale=plane,
+                start=(g == 0),
+                stop=(g == PASSES - 1),
+            )
+
+        acc_q = [sums.tile([P, N_TILE], F32, name="acc_q%d" % c) for c in range(Q_TILES)]
+        for g in range(PASSES):
+            wq_tile = wq_pool.tile([P, Q_COLS], U32, align_bytes=64)
+            nc.sync.dma_start(
+                out=wq_tile[:].bitcast(I32), in_=wq_words[g].rearrange("p n t -> p (n t)").bitcast(I32)
+            )
+            group, offset = g // PLANES_PER_TILE, SCALE_ROWS * (g % PLANES_PER_TILE)
+            for c in range(Q_TILES):
+                cols = slice(c * N_TILE, (c + 1) * N_TILE)
+                mx_pass(acc_q[c], g, wq_tile[:, cols], q_planes[offset:P, group, cols])
+
+        q_rot = keep.tile([P, Q_COLS], F32)
+        for c in range(Q_TILES):
+            rotate(nc, work, acc_q[c], cos_pairs, sin_signed, q_rot[:, c * N_TILE : (c + 1) * N_TILE])
+        nc.scalar.dma_start(out=out_0.rearrange("b s h d -> (b s) (h d)"), in_=q_rot[:])
+
+        def project(words_in, offset, name):
+            acc = sums.tile([P, N_TILE], F32, name=name)
+            for g in range(PASSES):
+                kv_tile = kv_pool.tile([P, N_TILE], U32, align_bytes=64)
+                nc.sync.dma_start(
+                    out=kv_tile[:].bitcast(I32), in_=words_in[g].rearrange("p n t -> p (n t)").bitcast(I32)
+                )
+                mx_pass(acc, g, kv_tile[:], kv_planes[offset:P, g, :])
+            return acc
+
+        acc_k = project(wk_words, K_OFFSET, "acc_k")
+        k_rot = keep.tile([P, N_TILE], F32)
+        rotate(nc, work, acc_k, cos_pairs, sin_signed, k_rot[:])
+        nc.scalar.dma_start(out=out_1.rearrange("b s h d -> (b s) (h d)"), in_=k_rot[:])
+
+        acc_v = project(wv_words, V_OFFSET, "acc_v")
+        v_sb = keep.tile([P, N_TILE], F32)
+        nc.scalar.copy(out=v_sb[:], in_=acc_v[:])
+        nc.scalar.dma_start(out=out_2.rearrange("b s h d -> (b s) (h d)"), in_=v_sb[:])

@@ -43,12 +43,7 @@ KV_BUFS = 16
 FLOPS = 2 * TOKENS * D_MODEL * (Q_COLS + 2 * N_TILE)
 
 
-def build_rope_tables(nc, keep):
-    position = keep.tile([P, 1], F32)
-    nc.gpsimd.iota(
-        position[:], pattern=[[0, 1]], base=0, channel_multiplier=1, allow_small_or_imprecise_dtypes=True
-    )
-
+def build_rope_tables(nc, keep, position):
     ratio = ROPE_THETA ** (-2.0 / HEAD)
     frequency = keep.tile([P, PAIRS], F32)
     nc.vector.memset(frequency[:, 0:1], 1.0)
@@ -102,31 +97,25 @@ def finish_cos_table(nc, keep, sin_half):
     return cos_pairs
 
 
-def load_scale_planes(nc, keep, wq_scales, wk_scales, wv_scales):
-    q_planes = keep.tile([P, PASSES // PLANES_PER_TILE, Q_COLS], U8, align_bytes=64)
-    kv_planes = keep.tile([P, PASSES, N_TILE], U8, align_bytes=64)
-    nc.vector.memset(q_planes[:].bitcast(I32), 0)
-    nc.vector.memset(kv_planes[:].bitcast(I32), 0)
-
+def load_scale_planes(nc, q_planes, kv_planes, wq_scales, wk_scales, wv_scales):
     rows = PLANES_PER_TILE * SCALE_ROWS
     for group in range(PASSES // PLANES_PER_TILE):
         for quadrant in range(QUADRANTS):
-            nc.sync.dma_start(
-                out=q_planes[32 * quadrant : 32 * quadrant + rows, group, :].bitcast(I32),
+            nc.gpsimd.dma_start(
+                out=q_planes[32 * quadrant : 32 * quadrant + rows, group, :].bitcast(F32),
                 in_=wq_scales[
                     PLANES_PER_TILE * group : PLANES_PER_TILE * (group + 1),
                     SCALE_ROWS * quadrant : SCALE_ROWS * (quadrant + 1),
                     :,
-                ].bitcast(I32),
+                ].bitcast(F32),
             )
     for scales, offset in ((wk_scales, K_OFFSET), (wv_scales, V_OFFSET)):
         by_row = scales.rearrange("g (quadrant r) n -> r quadrant g n", r=SCALE_ROWS)
         for r in range(SCALE_ROWS):
-            nc.sync.dma_start(
-                out=kv_planes[offset + r : P : 32, :, :].bitcast(I32),
-                in_=by_row[r].bitcast(I32),
+            nc.gpsimd.dma_start(
+                out=kv_planes[offset + r : P : 32, :, :].bitcast(F32),
+                in_=by_row[r].bitcast(F32),
             )
-    return q_planes, kv_planes
 
 
 def quantise_x(nc, keep, transposed, x_sb, identity):
@@ -199,11 +188,21 @@ def tile_rptattention_pa_k_kernel(
 
         x_sb = keep.tile([P, D_MODEL], BF16)
         nc.sync.dma_start(out=x_sb[:], in_=hidden_states.rearrange("b s d -> (b s) d"))
-        q_planes, kv_planes = load_scale_planes(nc, keep, wq_scales, wk_scales, wv_scales)
+
+        q_planes = keep.tile([P, PASSES // PLANES_PER_TILE, Q_COLS], U8, align_bytes=64)
+        kv_planes = keep.tile([P, PASSES, N_TILE], U8, align_bytes=64)
+        nc.vector.memset(q_planes[:].bitcast(I32), 0)
+        nc.vector.memset(kv_planes[:].bitcast(I32), 0)
 
         identity = keep.tile([P, P], F32)
         make_identity(nc, identity[:])
-        sin_signed, sin_half = build_rope_tables(nc, keep)
+        position = keep.tile([P, 1], F32)
+        nc.gpsimd.iota(
+            position[:], pattern=[[0, 1]], base=0, channel_multiplier=1, allow_small_or_imprecise_dtypes=True
+        )
+        load_scale_planes(nc, q_planes, kv_planes, wq_scales, wk_scales, wv_scales)
+
+        sin_signed, sin_half = build_rope_tables(nc, keep, position)
         x_codes, x_planes = quantise_x(nc, keep, transposed, x_sb, identity)
         cos_pairs = finish_cos_table(nc, keep, sin_half)
 

@@ -37,8 +37,8 @@ V_OFFSET = 4
 PASSES_PER_QUANTISE = 4
 ROUND_MAGIC = 12582912.0
 
-WQ_BUFS = 12
-KV_BUFS = 16
+OPERANDS_PER_LOAD = 4
+WEIGHT_BUFS = 16
 
 FLOPS = 2 * TOKENS * D_MODEL * (Q_COLS + 2 * N_TILE)
 
@@ -181,8 +181,7 @@ def tile_rptattention_pa_k_kernel(
         ctx.enter_context(tc.manual_schedule())
         keep = ctx.enter_context(tc.tile_pool(name="keep", bufs=1))
         work = ctx.enter_context(tc.tile_pool(name="work", bufs=2))
-        wq_pool = ctx.enter_context(tc.tile_pool(name="wq", bufs=WQ_BUFS))
-        kv_pool = ctx.enter_context(tc.tile_pool(name="kv", bufs=KV_BUFS))
+        weights = ctx.enter_context(tc.tile_pool(name="weights", bufs=WEIGHT_BUFS))
         sums = ctx.enter_context(tc.psum_pool(name="sums", bufs=1))
         transposed = ctx.enter_context(tc.psum_pool(name="transposed", bufs=2))
 
@@ -217,38 +216,41 @@ def tile_rptattention_pa_k_kernel(
                 stop=(g == PASSES - 1),
             )
 
+        def load_words(source, count):
+            w_tile = weights.tile([P, OPERANDS_PER_LOAD, N_TILE], U32, align_bytes=64)
+            nc.sync.dma_start(out=w_tile[:, 0:count, :].bitcast(I32), in_=source.bitcast(I32))
+            return w_tile
+
         acc_q = [sums.tile([P, N_TILE], F32, name="acc_q%d" % c) for c in range(Q_TILES)]
         for g in range(PASSES):
-            wq_tile = wq_pool.tile([P, Q_COLS], U32, align_bytes=64)
-            nc.sync.dma_start(
-                out=wq_tile[:].bitcast(I32), in_=wq_words[g].rearrange("p n t -> p (n t)").bitcast(I32)
-            )
+            w_tile = load_words(wq_words[g].rearrange("p (c n) t -> p c (n t)", c=Q_TILES), Q_TILES)
             group, offset = g // PLANES_PER_TILE, SCALE_ROWS * (g % PLANES_PER_TILE)
             for c in range(Q_TILES):
                 cols = slice(c * N_TILE, (c + 1) * N_TILE)
-                mx_pass(acc_q[c], g, wq_tile[:, cols], q_planes[offset:P, group, cols])
+                mx_pass(acc_q[c], g, w_tile[:, c, :], q_planes[offset:P, group, cols])
 
         q_rot = keep.tile([P, Q_COLS], F32)
         for c in range(Q_TILES):
             rotate(nc, work, acc_q[c], cos_pairs, sin_signed, q_rot[:, c * N_TILE : (c + 1) * N_TILE])
         nc.scalar.dma_start(out=out_0.rearrange("b s h d -> (b s) (h d)"), in_=q_rot[:])
 
-        def project(words_in, offset, name):
+        def project(words_in, offset, name, single_from):
             acc = sums.tile([P, N_TILE], F32, name=name)
-            for g in range(PASSES):
-                kv_tile = kv_pool.tile([P, N_TILE], U32, align_bytes=64)
-                nc.sync.dma_start(
-                    out=kv_tile[:].bitcast(I32), in_=words_in[g].rearrange("p n t -> p (n t)").bitcast(I32)
-                )
-                mx_pass(acc, g, kv_tile[:], kv_planes[offset:P, g, :])
+            g = 0
+            while g < PASSES:
+                count = OPERANDS_PER_LOAD if g < single_from else 1
+                w_tile = load_words(words_in[g : g + count].rearrange("g p n t -> p g (n t)"), count)
+                for i in range(count):
+                    mx_pass(acc, g + i, w_tile[:, i, :], kv_planes[offset:P, g + i, :])
+                g += count
             return acc
 
-        acc_k = project(wk_words, K_OFFSET, "acc_k")
+        acc_k = project(wk_words, K_OFFSET, "acc_k", PASSES)
         k_rot = keep.tile([P, N_TILE], F32)
         rotate(nc, work, acc_k, cos_pairs, sin_signed, k_rot[:])
         nc.scalar.dma_start(out=out_1.rearrange("b s h d -> (b s) (h d)"), in_=k_rot[:])
 
-        acc_v = project(wv_words, V_OFFSET, "acc_v")
+        acc_v = project(wv_words, V_OFFSET, "acc_v", PASSES - OPERANDS_PER_LOAD)
         v_sb = keep.tile([P, N_TILE], F32)
         nc.scalar.copy(out=v_sb[:], in_=acc_v[:])
         nc.scalar.dma_start(out=out_2.rearrange("b s h d -> (b s) (h d)"), in_=v_sb[:])

@@ -232,7 +232,6 @@ def tile_rptattention_pa_k_kernel(
         q_rot = keep.tile([P, Q_COLS], F32)
         for c in range(Q_TILES):
             rotate(nc, work, acc_q[c], cos_pairs, sin_signed, q_rot[:, c * N_TILE : (c + 1) * N_TILE])
-        nc.scalar.dma_start(out=out_0.rearrange("b s h d -> (b s) (h d)"), in_=q_rot[:])
 
         def project(words_in, offset, name, single_from):
             acc = sums.tile([P, N_TILE], F32, name=name)
@@ -248,9 +247,10 @@ def tile_rptattention_pa_k_kernel(
         acc_k = project(wk_words, K_OFFSET, "acc_k", PASSES)
         k_rot = keep.tile([P, N_TILE], F32)
         rotate(nc, work, acc_k, cos_pairs, sin_signed, k_rot[:])
-        nc.scalar.dma_start(out=out_1.rearrange("b s h d -> (b s) (h d)"), in_=k_rot[:])
 
         acc_v = project(wv_words, V_OFFSET, "acc_v", PASSES - OPERANDS_PER_LOAD)
+        nc.sync.dma_start(out=out_0.rearrange("b s h d -> (b s) (h d)"), in_=q_rot[:])
+        nc.sync.dma_start(out=out_1.rearrange("b s h d -> (b s) (h d)"), in_=k_rot[:])
         v_sb = keep.tile([P, N_TILE], F32)
         nc.scalar.copy(out=v_sb[:], in_=acc_v[:])
         nc.scalar.dma_start(out=out_2.rearrange("b s h d -> (b s) (h d)"), in_=v_sb[:])

@@ -33,6 +33,8 @@ QUADRANTS = 4
 PLANES_PER_TILE = 4
 K_OFFSET = 0
 V_OFFSET = 4
+KV_BLOCKS = PASSES // 2
+UPPER_HALF_OFFSET = 8
 
 PASSES_PER_QUANTISE = 4
 ROUND_MAGIC = 12582912.0
@@ -110,12 +112,15 @@ def load_scale_planes(nc, q_planes, kv_planes, wq_scales, wk_scales, wv_scales):
                 ].bitcast(F32),
             )
     for scales, offset in ((wk_scales, K_OFFSET), (wv_scales, V_OFFSET)):
-        by_row = scales.rearrange("g (quadrant r) n -> r quadrant g n", r=SCALE_ROWS)
-        for r in range(SCALE_ROWS):
-            nc.gpsimd.dma_start(
-                out=kv_planes[offset + r : P : 32, :, :].bitcast(F32),
-                in_=by_row[r].bitcast(F32),
+        for half in range(2):
+            by_row = scales[KV_BLOCKS * half : KV_BLOCKS * (half + 1)].rearrange(
+                "g (quadrant r) n -> r quadrant g n", r=SCALE_ROWS
             )
+            for r in range(SCALE_ROWS):
+                nc.gpsimd.dma_start(
+                    out=kv_planes[offset + UPPER_HALF_OFFSET * half + r : P : 32, :, :].bitcast(F32),
+                    in_=by_row[r].bitcast(F32),
+                )
 
 
 def quantise_x(nc, keep, transposed, x_sb, identity):
@@ -189,7 +194,7 @@ def tile_rptattention_pa_k_kernel(
         nc.sync.dma_start(out=x_sb[:], in_=hidden_states.rearrange("b s d -> (b s) d"))
 
         q_planes = keep.tile([P, PASSES // PLANES_PER_TILE, Q_COLS], U8, align_bytes=64)
-        kv_planes = keep.tile([P, PASSES, N_TILE], U8, align_bytes=64)
+        kv_planes = keep.tile([P, KV_BLOCKS, N_TILE], U8, align_bytes=64)
         nc.vector.memset(q_planes[:].bitcast(I32), 0)
         nc.vector.memset(kv_planes[:].bitcast(I32), 0)
 
@@ -240,7 +245,8 @@ def tile_rptattention_pa_k_kernel(
                 count = OPERANDS_PER_LOAD if g < single_from else 1
                 w_tile = load_words(words_in[g : g + count].rearrange("g p n t -> p g (n t)"), count)
                 for i in range(count):
-                    mx_pass(acc, g + i, w_tile[:, i, :], kv_planes[offset:P, g + i, :])
+                    first = offset + UPPER_HALF_OFFSET * ((g + i) // KV_BLOCKS)
+                    mx_pass(acc, g + i, w_tile[:, i, :], kv_planes[first:P, (g + i) % KV_BLOCKS, :])
                 g += count
             return acc
 

@@ -259,4 +259,4 @@ def tile_rptattention_pa_k_kernel(
         nc.sync.dma_start(out=out_1.rearrange("b s h d -> (b s) (h d)"), in_=k_rot[:])
         v_sb = keep.tile([P, N_TILE], F32)
         nc.scalar.copy(out=v_sb[:], in_=acc_v[:])
-        nc.scalar.dma_start(out=out_2.rearrange("b s h d -> (b s) (h d)"), in_=v_sb[:])
+        nc.sync.dma_start(out=out_2.rearrange("b s h d -> (b s) (h d)"), in_=v_sb[:])

import math
from contextlib import ExitStack

import concourse.mybir as mybir
from concourse.masks import make_identity

F32 = mybir.dt.float32
BF16 = mybir.dt.bfloat16
I32 = mybir.dt.int32
U32 = mybir.dt.uint32
U8 = mybir.dt.uint8
FP8X4 = mybir.dt.float8_e4m3fn_x4
ALU = mybir.AluOpType
ACT = mybir.ActivationFunctionType

P = 128
PACK = 4
K_PASS = P * PACK
TOKENS = 128
D_MODEL = 8192
PASSES = D_MODEL // K_PASS
WORDS_PER_PASS = K_PASS // 2
N_TILE = 512
HEAD = 128
PAIRS = HEAD // 2
HEADS_PER_TILE = N_TILE // HEAD
Q_COLS = 2048
Q_TILES = Q_COLS // N_TILE
ROPE_THETA = 10000.0

SCALE_ROWS = 4
QUADRANTS = 4
PLANES_PER_TILE = 4
K_OFFSET = 0
V_OFFSET = 4
KV_BLOCKS = PASSES // 2
UPPER_HALF_OFFSET = 8

PASSES_PER_QUANTISE = 4
ROUND_MAGIC = 12582912.0

OPERANDS_PER_LOAD = 4
WEIGHT_BUFS = 16

FLOPS = 2 * TOKENS * D_MODEL * (Q_COLS + 2 * N_TILE)


def build_rope_tables(nc, keep, position):
    ratio = ROPE_THETA ** (-2.0 / HEAD)
    frequency = keep.tile([P, PAIRS], F32)
    nc.vector.memset(frequency[:, 0:1], 1.0)
    filled = 1
    while filled < PAIRS:
        nc.vector.tensor_scalar(
            out=frequency[:, filled : 2 * filled],
            in0=frequency[:, 0:filled],
            scalar1=ratio**filled,
            scalar2=None,
            op0=ALU.mult,
        )
        filled *= 2

    angle = keep.tile([P, PAIRS], F32)
    nc.vector.tensor_scalar(
        out=angle[:],
        in0=frequency[:],
        scalar1=position[:, 0:1],
        scalar2=1.0 / (2.0 * math.pi),
        op0=ALU.mult,
        op1=ALU.mult,
    )
    whole = keep.tile([P, PAIRS], F32)
    nc.vector.tensor_scalar(
        out=whole[:], in0=angle[:], scalar1=ROUND_MAGIC, scalar2=ROUND_MAGIC, op0=ALU.add, op1=ALU.subtract
    )
    fraction = keep.tile([P, PAIRS], F32)
    nc.vector.tensor_tensor(out=fraction[:], in0=angle[:], in1=whole[:], op=ALU.subtract)

    sin_signed = keep.tile([P, 2, PAIRS], F32)
    nc.scalar.activation(out=sin_signed[:, 0, :], in_=fraction[:], func=ACT.Sin, scale=-2.0 * math.pi)
    nc.scalar.activation(out=sin_signed[:, 1, :], in_=fraction[:], func=ACT.Sin, scale=2.0 * math.pi)
    sin_half = keep.tile([P, PAIRS], F32)
    nc.scalar.activation(out=sin_half[:], in_=fraction[:], func=ACT.Sin, scale=math.pi)
    return sin_signed, sin_half


def finish_cos_table(nc, keep, sin_half):
    sin_half_sq = keep.tile([P, PAIRS], F32)
    nc.vector.tensor_tensor(out=sin_half_sq[:], in0=sin_half[:], in1=sin_half[:], op=ALU.mult)
    cos_pairs = keep.tile([P, HEAD], F32)
    nc.vector.tensor_scalar(
        out=cos_pairs[:].rearrange("p (j e) -> p j e", e=2),
        in0=sin_half_sq[:].unsqueeze(2).to_broadcast([P, PAIRS, 2]),
        scalar1=-2.0,
        scalar2=1.0,
        op0=ALU.mult,
        op1=ALU.add,
    )
    return cos_pairs


def load_scale_planes(nc, q_planes, kv_planes, wq_scales, wk_scales, wv_scales):
    rows = PLANES_PER_TILE * SCALE_ROWS
    for group in range(PASSES // PLANES_PER_TILE):
        for quadrant in range(QUADRANTS):
            nc.gpsimd.dma_start(
                out=q_planes[32 * quadrant : 32 * quadrant + rows, group, :].bitcast(F32),
                in_=wq_scales[
                    PLANES_PER_TILE * group : PLANES_PER_TILE * (group + 1),
                    SCALE_ROWS * quadrant : SCALE_ROWS * (quadrant + 1),
                    :,
                ].bitcast(F32),
            )
    for scales, offset in ((wk_scales, K_OFFSET), (wv_scales, V_OFFSET)):
        for half in range(2):
            by_row = scales[KV_BLOCKS * half : KV_BLOCKS * (half + 1)].rearrange(
                "g (quadrant r) n -> r quadrant g n", r=SCALE_ROWS
            )
            for r in range(SCALE_ROWS):
                nc.gpsimd.dma_start(
                    out=kv_planes[offset + UPPER_HALF_OFFSET * half + r : P : 32, :, :].bitcast(F32),
                    in_=by_row[r].bitcast(F32),
                )


def quantise_x(nc, keep, transposed, x_sb, identity):
    x_words = x_sb[:].bitcast(F32)
    grouped = keep.tile([P, PASSES, TOKENS * PACK], BF16, align_bytes=64)
    grouped_words = grouped[:].bitcast(F32)
    x_codes = keep.tile([P, PASSES, TOKENS], U32, align_bytes=64)
    x_planes = keep.tile([P, PASSES, TOKENS], U8, align_bytes=64)

    for first in range(0, PASSES, PASSES_PER_QUANTISE):
        for pair in range(first, first + PASSES_PER_QUANTISE, 2):
            bank = transposed.tile([P, 2, 2, TOKENS], F32)
            for a in range(2):
                start = WORDS_PER_PASS * (pair + a)
                for u in range(2):
                    nc.tensor.transpose(
                        bank[:, a, u, :], x_words[:, start + u : start + WORDS_PER_PASS : 2], identity[:]
                    )
            side_by_side = grouped_words[:, pair : pair + 2, :].rearrange("p a (t u) -> p a t u", u=2)
            if pair % 4 == 0:
                nc.vector.tensor_copy(out=side_by_side, in_=bank[:].rearrange("p a u t -> p a t u"))
            else:
                nc.scalar.copy(out=side_by_side, in_=bank[:].rearrange("p a u t -> p a t u"))
        these = slice(first, first + PASSES_PER_QUANTISE)
        nc.vector.quantize_mx(
            out=x_codes[:, these, :].rearrange("p g t -> p (g t)").bitcast(FP8X4),
            scales=x_planes[:, these, :].rearrange("p g t -> p (g t)"),
            in_=grouped[:, these, :].rearrange("p g c -> p (g c)"),
        )
    return x_codes, x_planes


def rotate(nc, work, acc, cos_pairs, sin_signed, rotated):
    with_cos = work.tile([P, N_TILE], F32)
    nc.vector.tensor_tensor(
        out=with_cos[:].rearrange("p (h d) -> p h d", d=HEAD),
        in0=acc[:].rearrange("p (h d) -> p h d", d=HEAD),
        in1=cos_pairs[:].unsqueeze(1).to_broadcast([P, HEADS_PER_TILE, HEAD]),
        op=ALU.mult,
    )
    acc_planes = acc[:].rearrange("p (h j e) -> p e h j", j=PAIRS, e=2)
    with_sin = work.tile([P, 2, HEADS_PER_TILE, PAIRS], F32)
    for e in range(2):
        nc.vector.tensor_tensor(
            out=with_sin[:, e, :, :],
            in0=acc_planes[:, 1 - e, :, :],
            in1=sin_signed[:, e, :].unsqueeze(1).to_broadcast([P, HEADS_PER_TILE, PAIRS]),
            op=ALU.mult,
        )
    nc.vector.tensor_tensor(
        out=rotated.rearrange("p (m e) -> p m e", e=2),
        in0=with_cos[:].rearrange("p (m e) -> p m e", e=2),
        in1=with_sin[:].rearrange("p e h j -> p (h j) e"),
        op=ALU.add,
    )


def tile_rptattention_pa_k_kernel(
    tc, hidden_states, wq_words, wq_scales, wk_words, wk_scales, wv_words, wv_scales, out_0, out_1, out_2
):
    nc = tc.nc
    with ExitStack() as ctx:
        ctx.enter_context(tc.manual_schedule())
        keep = ctx.enter_context(tc.tile_pool(name="keep", bufs=1))
        work = ctx.enter_context(tc.tile_pool(name="work", bufs=2))
        weights = ctx.enter_context(tc.tile_pool(name="weights", bufs=WEIGHT_BUFS))
        sums = ctx.enter_context(tc.psum_pool(name="sums", bufs=1))
        transposed = ctx.enter_context(tc.psum_pool(name="transposed", bufs=2))

        x_sb = keep.tile([P, D_MODEL], BF16)
        nc.sync.dma_start(out=x_sb[:], in_=hidden_states.rearrange("b s d -> (b s) d"))

        q_planes = keep.tile([P, PASSES // PLANES_PER_TILE, Q_COLS], U8, align_bytes=64)
        kv_planes = keep.tile([P, KV_BLOCKS, N_TILE], U8, align_bytes=64)
        nc.vector.memset(q_planes[:].bitcast(I32), 0)
        nc.vector.memset(kv_planes[:].bitcast(I32), 0)

        identity = keep.tile([P, P], F32)
        make_identity(nc, identity[:])
        position = keep.tile([P, 1], F32)
        nc.gpsimd.iota(
            position[:], pattern=[[0, 1]], base=0, channel_multiplier=1, allow_small_or_imprecise_dtypes=True
        )
        load_scale_planes(nc, q_planes, kv_planes, wq_scales, wk_scales, wv_scales)

        sin_signed, sin_half = build_rope_tables(nc, keep, position)
        x_codes, x_planes = quantise_x(nc, keep, transposed, x_sb, identity)
        cos_pairs = finish_cos_table(nc, keep, sin_half)

        def mx_pass(acc, g, words, plane):
            nc.tensor.matmul_mx(
                out=acc[:],
                lhsT=x_codes[:, g, :].bitcast(FP8X4),
                lhsT_scale=x_planes[:, g, :],
                rhs=words.bitcast(FP8X4),
                rhs_scale=plane,
                start=(g == 0),
                stop=(g == PASSES - 1),
            )

        def load_words(source, count):
            w_tile = weights.tile([P, OPERANDS_PER_LOAD, N_TILE], U32, align_bytes=64)
            nc.sync.dma_start(out=w_tile[:, 0:count, :].bitcast(I32), in_=source.bitcast(I32))
            return w_tile

        acc_q = [sums.tile([P, N_TILE], F32, name="acc_q%d" % c) for c in range(Q_TILES)]
        for g in range(PASSES):
            w_tile = load_words(wq_words[g].rearrange("p (c n) t -> p c (n t)", c=Q_TILES), Q_TILES)
            group, offset = g // PLANES_PER_TILE, SCALE_ROWS * (g % PLANES_PER_TILE)
            for c in range(Q_TILES):
                cols = slice(c * N_TILE, (c + 1) * N_TILE)
                mx_pass(acc_q[c], g, w_tile[:, c, :], q_planes[offset:P, group, cols])

        q_rot = keep.tile([P, Q_COLS], F32)
        for c in range(Q_TILES):
            rotate(nc, work, acc_q[c], cos_pairs, sin_signed, q_rot[:, c * N_TILE : (c + 1) * N_TILE])

        def project(words_in, offset, name, single_from):
            acc = sums.tile([P, N_TILE], F32, name=name)
            g = 0
            while g < PASSES:
                count = OPERANDS_PER_LOAD if g < single_from else 1
                w_tile = load_words(words_in[g : g + count].rearrange("g p n t -> p g (n t)"), count)
                for i in range(count):
                    first = offset + UPPER_HALF_OFFSET * ((g + i) // KV_BLOCKS)
                    mx_pass(acc, g + i, w_tile[:, i, :], kv_planes[first:P, (g + i) % KV_BLOCKS, :])
                g += count
            return acc

        acc_k = project(wk_words, K_OFFSET, "acc_k", PASSES)
        k_rot = keep.tile([P, N_TILE], F32)
        rotate(nc, work, acc_k, cos_pairs, sin_signed, k_rot[:])

        acc_v = project(wv_words, V_OFFSET, "acc_v", PASSES - OPERANDS_PER_LOAD)
        nc.sync.dma_start(out=out_0.rearrange("b s h d -> (b s) (h d)"), in_=q_rot[:])
        nc.sync.dma_start(out=out_1.rearrange("b s h d -> (b s) (h d)"), in_=k_rot[:])
        v_sb = keep.tile([P, N_TILE], F32)
        nc.scalar.copy(out=v_sb[:], in_=acc_v[:])
        nc.sync.dma_start(out=out_2.rearrange("b s h d -> (b s) (h d)"), in_=v_sb[:])
